import numpy as np
import ml_dtypes


def mxq(x, axis, fmt="e4m3"):
    dtype, down = {"e4m3": (ml_dtypes.float8_e4m3fn, 7), "e5m2": (ml_dtypes.float8_e5m2, 14)}[fmt]
    v = np.moveaxis(np.asarray(x, np.float32).astype(ml_dtypes.bfloat16).astype(np.float64), axis, -1)
    blocks = v.reshape(v.shape[:-1] + (-1, 32))
    amax = np.abs(blocks).max(-1, keepdims=True)
    byte = np.maximum(np.where(amax > 0, np.frexp(amax)[1] - 1 + 127, 0) - down, 1)
    scale = np.exp2(byte - 127.0)
    codes = (blocks / scale).astype(np.float32).astype(dtype).astype(np.float64)
    return np.moveaxis((codes * scale).reshape(v.shape), -1, axis)


WIDE = False


def mx_kscale(k):
    if not WIDE:
        return np.ones(k)
    levels = np.array([10, -10, 5, -5, 0])
    a = np.random.permutation(np.resize(levels, k // 512 * 4)).reshape(k // 512, 4)
    idx = np.arange(k)
    return np.exp2(a[idx // 512, idx % 128 // 32])


BF16 = ml_dtypes.bfloat16


def bf(x):
    return np.asarray(x, np.float32).astype(BF16)


def f64(x):
    return np.asarray(x).astype(np.float64)


E2M1 = np.array([0.0, 0.5, 1.0, 1.5, 2.0, 3.0, 4.0, 6.0, -0.0, -0.5, -1.0, -1.5, -2.0, -3.0, -4.0, -6.0])


def pack_weight(w, fmt):
    k, n = w.shape
    w = f64(bf(w)).reshape(k // 32, 32, n)
    amax = np.abs(w).max(1)
    if fmt == "e4m3":
        byte = np.frexp(amax)[1] - 1 + 127 - 7
    else:
        mant, ex = np.frexp(amax / 6.0)
        byte = np.where(mant > 0.5, ex, ex - 1) + 127
    byte = np.clip(np.where(amax > 0, byte, 1), 1, 254)
    scaled = (w * np.exp2(127.0 - byte)[:, None, :]).reshape(k, n).astype(np.float32)
    by_word = np.ascontiguousarray(scaled.reshape(k // 512, 128, 4, n).transpose(0, 1, 3, 2))
    if fmt == "e4m3":
        words = by_word.astype(ml_dtypes.float8_e4m3fn).view(np.uint8)
    else:
        c = by_word.astype(ml_dtypes.float4_e2m1fn).view(np.uint8) & 0xF
        words = c[..., 0::2] | (c[..., 1::2] << 4)
    return np.ascontiguousarray(words), np.ascontiguousarray(byte.astype(np.uint8).reshape(k // 512, 16, n))


def unpack_weight(words, scales, fmt):
    g, p, n, _ = words.shape
    if fmt == "e4m3":
        vals = np.ascontiguousarray(words).view(ml_dtypes.float8_e4m3fn).astype(np.float64)
    else:
        nib = np.empty((g, p, n, 4), np.uint8)
        nib[..., 0::2] = words & 0xF
        nib[..., 1::2] = words >> 4
        vals = E2M1[nib]
    vals = vals * np.repeat(np.exp2(scales.astype(np.float64) - 127.0), 8, axis=1)[..., None]
    return vals.transpose(0, 1, 3, 2).reshape(g * 512, n)


B, N, D, H, HD, FF = 8, 1024, 1024, 2, 64, 4096
E = H * HD
EPS = 1e-5
FMT = "e4m3"


def layernorm(x, gamma, beta):
    mu = x.mean(-1, keepdims=True)
    var = ((x - mu) ** 2).mean(-1, keepdims=True)
    return (x - mu) * (1.0 / np.sqrt(var + EPS)) * gamma + beta


def heads(y):
    return y.reshape(B, N, H, HD).transpose(0, 2, 1, 3)


def setup_inputs():
    s = mx_kscale(D)
    r = np.random.standard_normal
    x = bf(r((B, N, D)))
    gamma = bf((1.0 + 0.1 * r(D)) * s)
    beta = bf(0.1 * r(D) * s)
    Wq_words, Wq_scales = pack_weight(r((D, E)) * 1.4 / np.sqrt(D) / s[:, None], FMT)
    bq = bf(r(E) * 0.2)
    Wk_words, Wk_scales = pack_weight(r((D, E)) * 1.4 / np.sqrt(D) / s[:, None], FMT)
    bk = bf(r(E) * 0.2)
    Wv_words, Wv_scales = pack_weight(r((D, E)) * 1.0 / np.sqrt(D) / s[:, None], FMT)
    bv = bf(r(E) * 0.2)
    return {"x": x,
            "gamma": gamma, "beta": beta,
            "Wq_words": Wq_words, "Wq_scales": Wq_scales, "bq": bq,
            "Wk_words": Wk_words, "Wk_scales": Wk_scales, "bk": bk,
            "Wv_words": Wv_words, "Wv_scales": Wv_scales, "bv": bv}


def reference(x, gamma, beta, Wq_words, Wq_scales, bq, Wk_words, Wk_scales, bk, Wv_words, Wv_scales, bv):
    h = layernorm(f64(x), f64(gamma), f64(beta))
    hq = mxq(h, 2, "e4m3")
    q = (hq @ unpack_weight(Wq_words, Wq_scales, FMT)) + f64(bq)
    k = (hq @ unpack_weight(Wk_words, Wk_scales, FMT)) + f64(bk)
    v = (hq @ unpack_weight(Wv_words, Wv_scales, FMT)) + f64(bv)
    return heads(q), heads(k), heads(v)

@@ -1,0 +1,260 @@
+from contextlib import ExitStack
+
+import concourse.mybir as mybir
+from concourse.masks import make_identity
+
+F32 = mybir.dt.float32
+BF16 = mybir.dt.bfloat16
+I32 = mybir.dt.int32
+U32 = mybir.dt.uint32
+U8 = mybir.dt.uint8
+FP8X4 = mybir.dt.float8_e4m3fn_x4
+ALU = mybir.AluOpType
+ACT = mybir.ActivationFunctionType
+
+P = 128
+BATCH, SEQ, D = 8, 1024, 1024
+HEADS, HEAD_DIM = 2, 64
+E = HEADS * HEAD_DIM
+EPS = 1e-5
+PACK = 4
+K_PASS = P * PACK
+PASSES = D // K_PASS
+PLANES = PASSES * PACK
+TILES = 4
+UNIT = P * TILES
+UNITS = BATCH * SEQ // UNIT
+UNITS_PER_BATCH = SEQ // UNIT
+BN_CHUNK = 512
+RUN = 4
+
+FLOPS = 2 * BATCH * SEQ * D * 3 * E
+
+
+def tile_vit_transformerblock_pa_t_kernel(
+    tc,
+    x,
+    gamma,
+    beta,
+    Wq_words,
+    Wq_scales,
+    bq,
+    Wk_words,
+    Wk_scales,
+    bk,
+    Wv_words,
+    Wv_scales,
+    bv,
+    out_0,
+    out_1,
+    out_2,
+):
+    nc = tc.nc
+    weights = ((Wq_words, Wq_scales), (Wk_words, Wk_scales), (Wv_words, Wv_scales))
+    x_units = x.flatten_outer_dims().rearrange("(u p j) k -> u p j k", p=P, j=TILES)
+    out_units = [
+        o.rearrange("b a (h p j) d -> b h p a (j d)", h=UNITS_PER_BATCH, p=P, j=TILES)
+        for o in (out_0, out_1, out_2)
+    ]
+
+    with ExitStack() as ctx:
+        const = ctx.enter_context(tc.tile_pool(name="const", bufs=1))
+        x_pool = ctx.enter_context(tc.tile_pool(name="x", bufs=4))
+        stat_pool = ctx.enter_context(tc.tile_pool(name="stat", bufs=3))
+        z_pool = ctx.enter_context(tc.tile_pool(name="z", bufs=2))
+        h_pool = ctx.enter_context(tc.tile_pool(name="h", bufs=2))
+        o_pool = ctx.enter_context(tc.tile_pool(name="o", bufs=2))
+        zt_pool = ctx.enter_context(tc.psum_pool(name="zt", bufs=5))
+        acc_pool = ctx.enter_context(tc.psum_pool(name="acc", bufs=1))
+
+        x_tiles, stats, z_tiles, h_tiles, acc_tiles = {}, {}, {}, {}, {}
+
+        def load(u):
+            x_sb = x_pool.tile([P, TILES, D], BF16, name="x_sb")
+            nc.sync.dma_start(out=x_sb[:], in_=x_units[u])
+            x_tiles[u] = x_sb
+
+        def load_constants():
+            identity = const.tile([P, P], F32, name="identity")
+            make_identity(nc, identity[:])
+            eps = const.tile([P, 1], F32, name="eps")
+            nc.vector.memset(eps[:], EPS)
+
+            affine = const.tile([P, 2, PLANES], F32, name="affine")
+            for i, vec in enumerate((gamma, beta)):
+                vec_bf = const.tile([P, PASSES, PACK], BF16, name="vec_bf%d" % i)
+                nc.scalar.dma_start(
+                    out=vec_bf[:], in_=vec.rearrange("(g p t) -> p g t", g=PASSES, p=P)
+                )
+                nc.vector.tensor_copy(
+                    out=affine[:, i, :], in_=vec_bf[:].rearrange("p g t -> p (g t)")
+                )
+
+            bias_bf = const.tile([P, 3, E], BF16, name="bias_bf")
+            for w, b in enumerate((bq, bk, bv)):
+                nc.scalar.dma_start(out=bias_bf[:, w, :], in_=b.partition_broadcast(P))
+            bias = const.tile([P, 3, 1, HEADS, HEAD_DIM], F32, name="bias")
+            nc.vector.tensor_copy(
+                out=bias[:].rearrange("p w o a d -> p w (o a d)"), in_=bias_bf[:]
+            )
+
+            w_codes = const.tile([P, 3, PASSES, E], U32, name="w_codes", align_bytes=64)
+            w_scales = const.tile([P, 3, PASSES, E], U8, name="w_scales", align_bytes=64)
+            nc.vector.memset(w_scales[:].rearrange("p w g n -> p (w g n)").bitcast(I32), 0)
+            for w, (words, scales) in enumerate(weights):
+                nc.sync.dma_start(
+                    out=w_codes[:, w].bitcast(I32),
+                    in_=words.rearrange("g p n t -> p g (n t)").bitcast(I32),
+                )
+                rows = scales.rearrange("g (Q r) n -> r Q g n", r=4)
+                for r in range(4):
+                    nc.sync.dma_start(
+                        out=w_scales[r:P:32, w].bitcast(I32), in_=rows[r].bitcast(I32)
+                    )
+            return identity, eps, affine, bias, w_codes, w_scales
+
+        def row_statistics(u):
+            x_sb = x_tiles[u]
+            chunks = D // BN_CHUNK
+            partial = stat_pool.tile([P, TILES, chunks, 6], F32, name="partial")
+            mean_var = stat_pool.tile([P, TILES, 2], F32, name="mean_var")
+            for j in range(TILES):
+                for c in range(chunks):
+                    nc.vector.bn_stats(
+                        out=partial[:, j, c, :], in_=x_sb[:, j, c * BN_CHUNK : (c + 1) * BN_CHUNK]
+                    )
+                nc.vector.bn_aggr(
+                    out=mean_var[:, j, :], in_=partial[:, j].rearrange("p c s -> p (c s)")
+                )
+            stats[u] = {"mean_var": mean_var}
+
+        def standard_deviation(u):
+            std = stat_pool.tile([P, TILES, 1], F32, name="std")
+            nc.scalar.activation(
+                out=std[:], in_=stats[u]["mean_var"][:, :, 1:2], func=ACT.Sqrt, bias=eps[:], scale=1.0
+            )
+            stats[u]["std"] = std
+
+        def row_scalars(u):
+            rstd = stat_pool.tile([P, TILES, 1], F32, name="rstd")
+            neg_mean = stat_pool.tile([P, TILES, 1], F32, name="neg_mean")
+            nc.vector.reciprocal(out=rstd[:], in_=stats[u]["std"][:])
+            nc.vector.tensor_scalar(
+                out=neg_mean[:],
+                in0=stats[u]["mean_var"][:, :, 0:1],
+                scalar1=-1.0,
+                scalar2=None,
+                op0=ALU.mult,
+            )
+            stats[u]["rstd"] = rstd
+            stats[u]["neg_mean"] = neg_mean
+
+        def normalise(u):
+            x_sb = x_tiles[u]
+            s = stats[u]
+            z = z_pool.tile([P, TILES, PASSES, PACK, P], F32, name="z")
+            for j in range(TILES):
+                nc.gpsimd.tensor_scalar(
+                    out=z[:, j],
+                    in0=x_sb[:, j, :].rearrange("r (g p t) -> r g t p", g=PASSES, t=PACK),
+                    scalar1=s["neg_mean"][:, j, :],
+                    scalar2=s["rstd"][:, j, :],
+                    op0=ALU.add,
+                    op1=ALU.mult,
+                )
+            z_tiles[u] = z
+
+        def transpose_and_scale(u):
+            z = z_tiles[u]
+            planes = h_pool.tile([P, PASSES, PACK, UNIT], BF16, name="planes")
+            for g in reversed(range(PASSES)):
+                for t in range(PACK):
+                    zt = zt_pool.tile([P, UNIT], F32, name="zt")
+                    for j in range(TILES):
+                        nc.tensor.transpose(
+                            out=zt[:, j * P : (j + 1) * P], in_=z[:, j, g, t, :], identity=identity[:]
+                        )
+                    plane = g * PACK + t
+                    nc.scalar.activation(
+                        out=planes[:, g, t, :],
+                        in_=zt[:],
+                        func=ACT.Identity,
+                        scale=affine[:, 0, plane : plane + 1],
+                        bias=affine[:, 1, plane : plane + 1],
+                    )
+            h_tiles[u] = {"planes": planes}
+
+        def regroup(u):
+            planes = h_tiles[u]["planes"]
+            grouped = h_pool.tile([P, PASSES, UNIT * PACK], BF16, name="grouped", align_bytes=64)
+            words_to_be = [
+                grouped[:, g, :].rearrange("p (c i t) -> p c t i", i=RUN, t=PACK)
+                for g in range(PASSES)
+            ]
+            by_plane = [planes[:, g].rearrange("p t (c i) -> p c t i", i=RUN) for g in range(PASSES)]
+            nc.vector.tensor_copy(out=words_to_be[0], in_=by_plane[0])
+            nc.scalar.copy(out=words_to_be[1], in_=by_plane[1])
+            h_tiles[u]["grouped"] = grouped
+
+        def quantise(u):
+            grouped = h_tiles[u]["grouped"]
+            codes = h_pool.tile([P, PASSES, UNIT], U32, name="codes", align_bytes=64)
+            scales = h_pool.tile([P, PASSES, UNIT], U8, name="scales", align_bytes=64)
+            for g in range(PASSES):
+                nc.vector.quantize_mx(
+                    out=codes[:, g, :].bitcast(FP8X4), scales=scales[:, g, :], in_=grouped[:, g, :]
+                )
+            h_tiles[u] = {"codes": codes, "scales": scales}
+
+        def project(u):
+            h = h_tiles[u]
+            acc_tiles[u] = []
+            for w in range(3):
+                acc = acc_pool.tile([P, TILES, E], F32, name="acc%d" % w)
+                for j in range(TILES):
+                    rows = slice(j * P, (j + 1) * P)
+                    for g in range(PASSES):
+                        nc.tensor.matmul_mx(
+                            out=acc[:, j, :],
+                            lhsT=h["codes"][:, g, rows].bitcast(FP8X4),
+                            lhsT_scale=h["scales"][:, g, rows],
+                            rhs=w_codes[:, w, g, :].bitcast(FP8X4),
+                            rhs_scale=w_scales[:, w, g, :],
+                            start=(g == 0),
+                            stop=(g == PASSES - 1),
+                        )
+                acc_tiles[u].append(acc)
+
+        def finish(u):
+            result = o_pool.tile([P, 3, HEADS, TILES, HEAD_DIM], F32, name="result")
+            for w, acc in enumerate(acc_tiles[u]):
+                nc.vector.tensor_tensor(
+                    out=result[:, w].rearrange("p a j d -> p j a d"),
+                    in0=acc[:].rearrange("p j (a d) -> p j a d", a=HEADS),
+                    in1=bias[:, w].to_broadcast([P, TILES, HEADS, HEAD_DIM]),
+                    op=ALU.add,
+                )
+                nc.sync.dma_start(
+                    out=out_units[w][u // UNITS_PER_BATCH, u % UNITS_PER_BATCH],
+                    in_=result[:, w].rearrange("p a j d -> p a (j d)"),
+                )
+
+        def run(stage, u):
+            if 0 <= u < UNITS:
+                stage(u)
+
+        with tc.manual_schedule():
+            load(0)
+            load(1)
+            identity, eps, affine, bias, w_codes, w_scales = load_constants()
+            for s in range(UNITS + 3):
+                run(load, s + 2)
+                run(row_scalars, s - 1)
+                run(normalise, s - 1)
+                run(row_statistics, s)
+                run(transpose_and_scale, s - 2)
+                run(regroup, s - 2)
+                run(standard_deviation, s)
+                run(project, s - 3)
+                run(finish, s - 3)
+                run(quantise, s - 2)

@@ -184,27 +184,29 @@ def tile_vit_transformerblock_pa_t_kernel(
                     )
             h_tiles[u] = {"planes": planes}
 
-        def regroup(u):
-            planes = h_tiles[u]["planes"]
-            grouped = h_pool.tile([P, PASSES, UNIT * PACK], BF16, name="grouped", align_bytes=64)
-            words_to_be = [
-                grouped[:, g, :].rearrange("p (c i t) -> p c t i", i=RUN, t=PACK)
-                for g in range(PASSES)
-            ]
-            by_plane = [planes[:, g].rearrange("p t (c i) -> p c t i", i=RUN) for g in range(PASSES)]
-            nc.vector.tensor_copy(out=words_to_be[0], in_=by_plane[0])
-            nc.scalar.copy(out=words_to_be[1], in_=by_plane[1])
-            h_tiles[u]["grouped"] = grouped
+        def regroup(copy, u, g):
+            grouped = h_pool.tile([P, UNIT * PACK], BF16, name="grouped%d" % g, align_bytes=64)
+            copy(
+                out=grouped[:].rearrange("p (c i t) -> p c t i", i=RUN, t=PACK),
+                in_=h_tiles[u]["planes"][:, g].rearrange("p t (c i) -> p c t i", i=RUN),
+            )
+            h_tiles[u][g] = grouped
+
+        def regroup_on_scalar(u):
+            regroup(nc.scalar.copy, u, 1)
+
+        def regroup_on_vector(u):
+            regroup(nc.vector.tensor_copy, u, 0)
 
         def quantise(u):
-            grouped = h_tiles[u]["grouped"]
             codes = h_pool.tile([P, PASSES, UNIT], U32, name="codes", align_bytes=64)
             scales = h_pool.tile([P, PASSES, UNIT], U8, name="scales", align_bytes=64)
-            for g in range(PASSES):
+            for g in reversed(range(PASSES)):
                 nc.vector.quantize_mx(
-                    out=codes[:, g, :].bitcast(FP8X4), scales=scales[:, g, :], in_=grouped[:, g, :]
+                    out=codes[:, g, :].bitcast(FP8X4), scales=scales[:, g, :], in_=h_tiles[u][g][:]
                 )
-            h_tiles[u] = {"codes": codes, "scales": scales}
+            h_tiles[u]["codes"] = codes
+            h_tiles[u]["scales"] = scales
 
         def project(u):
             h = h_tiles[u]
@@ -247,14 +249,15 @@ def tile_vit_transformerblock_pa_t_kernel(
             load(0)
             load(1)
             identity, eps, affine, bias, w_codes, w_scales = load_constants()
-            for s in range(UNITS + 3):
+            for s in range(UNITS + 4):
                 run(load, s + 2)
+                run(regroup_on_vector, s - 3)
+                run(quantise, s - 3)
                 run(row_scalars, s - 1)
                 run(normalise, s - 1)
+                run(finish, s - 4)
                 run(row_statistics, s)
                 run(transpose_and_scale, s - 2)
-                run(regroup, s - 2)
+                run(regroup_on_scalar, s - 2)
                 run(standard_deviation, s)
                 run(project, s - 3)
-                run(finish, s - 3)
-                run(quantise, s - 2)

@@ -123,31 +123,26 @@ def tile_vit_transformerblock_pa_t_kernel(
                     nc.vector.bn_stats(
                         out=partial[:, j, c, :], in_=x_sb[:, j, c * BN_CHUNK : (c + 1) * BN_CHUNK]
                     )
+            for j in range(TILES):
                 nc.vector.bn_aggr(
                     out=mean_var[:, j, :], in_=partial[:, j].rearrange("p c s -> p (c s)")
                 )
             stats[u] = {"mean_var": mean_var}
 
-        def standard_deviation(u):
+        def row_scalars(u):
             std = stat_pool.tile([P, TILES, 1], F32, name="std")
+            neg_mean = stat_pool.tile([P, TILES, 1], F32, name="neg_mean")
             nc.scalar.activation(
                 out=std[:], in_=stats[u]["mean_var"][:, :, 1:2], func=ACT.Sqrt, bias=eps[:], scale=1.0
             )
+            nc.scalar.mul(out=neg_mean[:], in_=stats[u]["mean_var"][:, :, 0:1], mul=-1.0)
             stats[u]["std"] = std
-
-        def row_scalars(u):
-            rstd = stat_pool.tile([P, TILES, 1], F32, name="rstd")
-            neg_mean = stat_pool.tile([P, TILES, 1], F32, name="neg_mean")
-            nc.vector.reciprocal(out=rstd[:], in_=stats[u]["std"][:])
-            nc.vector.tensor_scalar(
-                out=neg_mean[:],
-                in0=stats[u]["mean_var"][:, :, 0:1],
-                scalar1=-1.0,
-                scalar2=None,
-                op0=ALU.mult,
-            )
-            stats[u]["rstd"] = rstd
             stats[u]["neg_mean"] = neg_mean
+
+        def reciprocal_std(u):
+            rstd = stat_pool.tile([P, TILES, 1], F32, name="rstd")
+            nc.vector.reciprocal(out=rstd[:], in_=stats[u]["std"][:])
+            stats[u]["rstd"] = rstd
 
         def normalise(u):
             x_sb = x_tiles[u]
@@ -185,14 +180,15 @@ def tile_vit_transformerblock_pa_t_kernel(
             h_tiles[u] = {"planes": planes}
 
         def regroup(copy, u, g):
-            grouped = h_pool.tile([P, UNIT * PACK], BF16, name="grouped%d" % g, align_bytes=64)
             copy(
-                out=grouped[:].rearrange("p (c i t) -> p c t i", i=RUN, t=PACK),
+                out=h_tiles[u]["grouped"][:, g, :].rearrange("p (c i t) -> p c t i", i=RUN, t=PACK),
                 in_=h_tiles[u]["planes"][:, g].rearrange("p t (c i) -> p c t i", i=RUN),
             )
-            h_tiles[u][g] = grouped
 
         def regroup_on_scalar(u):
+            h_tiles[u]["grouped"] = h_pool.tile(
+                [P, PASSES, UNIT * PACK], BF16, name="grouped", align_bytes=64
+            )
             regroup(nc.scalar.copy, u, 1)
 
         def regroup_on_vector(u):
@@ -201,10 +197,11 @@ def tile_vit_transformerblock_pa_t_kernel(
         def quantise(u):
             codes = h_pool.tile([P, PASSES, UNIT], U32, name="codes", align_bytes=64)
             scales = h_pool.tile([P, PASSES, UNIT], U8, name="scales", align_bytes=64)
-            for g in reversed(range(PASSES)):
-                nc.vector.quantize_mx(
-                    out=codes[:, g, :].bitcast(FP8X4), scales=scales[:, g, :], in_=h_tiles[u][g][:]
-                )
+            nc.vector.quantize_mx(
+                out=codes[:].rearrange("p g c -> p (g c)").bitcast(FP8X4),
+                scales=scales[:].rearrange("p g c -> p (g c)"),
+                in_=h_tiles[u]["grouped"][:].rearrange("p g e -> p (g e)"),
+            )
             h_tiles[u]["codes"] = codes
             h_tiles[u]["scales"] = scales
 
@@ -252,12 +249,12 @@ def tile_vit_transformerblock_pa_t_kernel(
             for s in range(UNITS + 4):
                 run(load, s + 2)
                 run(regroup_on_vector, s - 3)
-                run(quantise, s - 3)
-                run(row_scalars, s - 1)
+                run(reciprocal_std, s - 1)
                 run(normalise, s - 1)
                 run(finish, s - 4)
+                run(quantise, s - 3)
                 run(row_statistics, s)
                 run(transpose_and_scale, s - 2)
                 run(regroup_on_scalar, s - 2)
-                run(standard_deviation, s)
+                run(row_scalars, s)
                 run(project, s - 3)

@@ -62,7 +62,7 @@ def tile_vit_transformerblock_pa_t_kernel(
         x_pool = ctx.enter_context(tc.tile_pool(name="x", bufs=4))
         stat_pool = ctx.enter_context(tc.tile_pool(name="stat", bufs=3))
         z_pool = ctx.enter_context(tc.tile_pool(name="z", bufs=2))
-        h_pool = ctx.enter_context(tc.tile_pool(name="h", bufs=2))
+        h_pool = ctx.enter_context(tc.tile_pool(name="h", bufs=3))
         o_pool = ctx.enter_context(tc.tile_pool(name="o", bufs=2))
         zt_pool = ctx.enter_context(tc.psum_pool(name="zt", bufs=5))
         acc_pool = ctx.enter_context(tc.psum_pool(name="acc", bufs=1))
@@ -246,15 +246,15 @@ def tile_vit_transformerblock_pa_t_kernel(
             load(0)
             load(1)
             identity, eps, affine, bias, w_codes, w_scales = load_constants()
-            for s in range(UNITS + 4):
+            for s in range(UNITS + 5):
                 run(load, s + 2)
+                run(quantise, s - 4)
                 run(regroup_on_vector, s - 3)
                 run(reciprocal_std, s - 1)
                 run(normalise, s - 1)
-                run(finish, s - 4)
-                run(quantise, s - 3)
+                run(finish, s - 5)
                 run(row_statistics, s)
                 run(transpose_and_scale, s - 2)
                 run(regroup_on_scalar, s - 2)
                 run(row_scalars, s)
-                run(project, s - 3)
+                run(project, s - 4)

@@ -27,6 +27,8 @@ UNITS = BATCH * SEQ // UNIT
 UNITS_PER_BATCH = SEQ // UNIT
 BN_CHUNK = 512
 RUN = 4
+VECTOR_COLUMNS = 256
+AHEAD = 4
 
 FLOPS = 2 * BATCH * SEQ * D * 3 * E
 
@@ -59,10 +61,10 @@ def tile_vit_transformerblock_pa_t_kernel(
 
     with ExitStack() as ctx:
         const = ctx.enter_context(tc.tile_pool(name="const", bufs=1))
-        x_pool = ctx.enter_context(tc.tile_pool(name="x", bufs=4))
-        stat_pool = ctx.enter_context(tc.tile_pool(name="stat", bufs=3))
+        x_pool = ctx.enter_context(tc.tile_pool(name="x", bufs=AHEAD + 2))
+        stat_pool = ctx.enter_context(tc.tile_pool(name="stat", bufs=4))
         z_pool = ctx.enter_context(tc.tile_pool(name="z", bufs=2))
-        h_pool = ctx.enter_context(tc.tile_pool(name="h", bufs=3))
+        h_pool = ctx.enter_context(tc.tile_pool(name="h", bufs=2))
         o_pool = ctx.enter_context(tc.tile_pool(name="o", bufs=2))
         zt_pool = ctx.enter_context(tc.psum_pool(name="zt", bufs=5))
         acc_pool = ctx.enter_context(tc.psum_pool(name="acc", bufs=1))
@@ -71,7 +73,8 @@ def tile_vit_transformerblock_pa_t_kernel(
 
         def load(u):
             x_sb = x_pool.tile([P, TILES, D], BF16, name="x_sb")
-            nc.sync.dma_start(out=x_sb[:], in_=x_units[u])
+            for j in range(TILES):
+                nc.sync.dma_start(out=x_sb[:, j, :], in_=x_units[u][:, j, :])
             x_tiles[u] = x_sb
 
         def load_constants():
@@ -161,7 +164,7 @@ def tile_vit_transformerblock_pa_t_kernel(
 
         def transpose_and_scale(u):
             z = z_tiles[u]
-            planes = h_pool.tile([P, PASSES, PACK, UNIT], BF16, name="planes")
+            planes = h_pool.tile([P, PASSES, PACK, UNIT], BF16, name="planes", bufs=AHEAD - 1)
             for g in reversed(range(PASSES)):
                 for t in range(PACK):
                     zt = zt_pool.tile([P, UNIT], F32, name="zt")
@@ -179,20 +182,23 @@ def tile_vit_transformerblock_pa_t_kernel(
                     )
             h_tiles[u] = {"planes": planes}
 
-        def regroup(copy, u, g):
+        def regroup(copy, u, g, first, last):
             copy(
-                out=h_tiles[u]["grouped"][:, g, :].rearrange("p (c i t) -> p c t i", i=RUN, t=PACK),
-                in_=h_tiles[u]["planes"][:, g].rearrange("p t (c i) -> p c t i", i=RUN),
+                out=h_tiles[u]["grouped"][:, g, first * PACK : last * PACK].rearrange(
+                    "p (c i t) -> p c t i", i=RUN, t=PACK
+                ),
+                in_=h_tiles[u]["planes"][:, g, :, first:last].rearrange("p t (c i) -> p c t i", i=RUN),
             )
 
         def regroup_on_scalar(u):
             h_tiles[u]["grouped"] = h_pool.tile(
-                [P, PASSES, UNIT * PACK], BF16, name="grouped", align_bytes=64
+                [P, PASSES, UNIT * PACK], BF16, name="grouped", align_bytes=64, bufs=AHEAD
             )
-            regroup(nc.scalar.copy, u, 1)
+            regroup(nc.scalar.copy, u, 1, 0, UNIT)
+            regroup(nc.scalar.copy, u, 0, VECTOR_COLUMNS, UNIT)
 
         def regroup_on_vector(u):
-            regroup(nc.vector.tensor_copy, u, 0)
+            regroup(nc.vector.tensor_copy, u, 0, 0, VECTOR_COLUMNS)
 
         def quantise(u):
             codes = h_pool.tile([P, PASSES, UNIT], U32, name="codes", align_bytes=64)
@@ -246,15 +252,15 @@ def tile_vit_transformerblock_pa_t_kernel(
             load(0)
             load(1)
             identity, eps, affine, bias, w_codes, w_scales = load_constants()
-            for s in range(UNITS + 5):
+            for s in range(UNITS + AHEAD + 2):
                 run(load, s + 2)
-                run(quantise, s - 4)
-                run(regroup_on_vector, s - 3)
+                run(quantise, s - AHEAD - 1)
+                run(regroup_on_vector, s - AHEAD)
                 run(reciprocal_std, s - 1)
                 run(normalise, s - 1)
-                run(finish, s - 5)
+                run(finish, s - AHEAD - 2)
                 run(row_statistics, s)
                 run(transpose_and_scale, s - 2)
-                run(regroup_on_scalar, s - 2)
                 run(row_scalars, s)
-                run(project, s - 4)
+                run(regroup_on_scalar, s - 2)
+                run(project, s - AHEAD - 1)

@@ -23,8 +23,9 @@ PASSES = D // K_PASS
 PLANES = PASSES * PACK
 TILES = 4
 UNIT = P * TILES
-UNITS = BATCH * SEQ // UNIT
-UNITS_PER_BATCH = SEQ // UNIT
+BLOCKS = BATCH * SEQ // UNIT
+BLOCKS_PER_BATCH = SEQ // UNIT
+FINE_BLOCKS = 2
 BN_CHUNK = 512
 RUN = 4
 VECTOR_COLUMNS = 256
@@ -55,9 +56,16 @@ def tile_vit_transformerblock_pa_t_kernel(
     weights = ((Wq_words, Wq_scales), (Wk_words, Wk_scales), (Wv_words, Wv_scales))
     x_units = x.flatten_outer_dims().rearrange("(u p j) k -> u p j k", p=P, j=TILES)
     out_units = [
-        o.rearrange("b a (h p j) d -> b h p a (j d)", h=UNITS_PER_BATCH, p=P, j=TILES)
+        o.rearrange("b a (h p j) d -> b h p a (j d)", h=BLOCKS_PER_BATCH, p=P, j=TILES)
         for o in (out_0, out_1, out_2)
     ]
+    units = []
+    for block in range(BLOCKS):
+        if block < FINE_BLOCKS or block >= BLOCKS - FINE_BLOCKS:
+            units.extend([(block, 0, TILES // 2), (block, TILES // 2, TILES // 2)])
+        else:
+            units.append((block, 0, TILES))
+    UNITS = len(units)
 
     with ExitStack() as ctx:
         const = ctx.enter_context(tc.tile_pool(name="const", bufs=1))
@@ -72,9 +80,10 @@ def tile_vit_transformerblock_pa_t_kernel(
         x_tiles, stats, z_tiles, h_tiles, acc_tiles = {}, {}, {}, {}, {}
 
         def load(u):
+            block, first, tiles = units[u]
             x_sb = x_pool.tile([P, TILES, D], BF16, name="x_sb")
-            for j in range(TILES):
-                nc.sync.dma_start(out=x_sb[:, j, :], in_=x_units[u][:, j, :])
+            for j in range(tiles):
+                nc.sync.dma_start(out=x_sb[:, j, :], in_=x_units[block][:, first + j, :])
             x_tiles[u] = x_sb
 
         def load_constants():
@@ -118,40 +127,49 @@ def tile_vit_transformerblock_pa_t_kernel(
 
         def row_statistics(u):
             x_sb = x_tiles[u]
+            tiles = units[u][2]
             chunks = D // BN_CHUNK
             partial = stat_pool.tile([P, TILES, chunks, 6], F32, name="partial")
             mean_var = stat_pool.tile([P, TILES, 2], F32, name="mean_var")
-            for j in range(TILES):
+            for j in range(tiles):
                 for c in range(chunks):
                     nc.vector.bn_stats(
                         out=partial[:, j, c, :], in_=x_sb[:, j, c * BN_CHUNK : (c + 1) * BN_CHUNK]
                     )
-            for j in range(TILES):
+            for j in range(tiles):
                 nc.vector.bn_aggr(
                     out=mean_var[:, j, :], in_=partial[:, j].rearrange("p c s -> p (c s)")
                 )
             stats[u] = {"mean_var": mean_var}
 
         def row_scalars(u):
+            tiles = units[u][2]
             std = stat_pool.tile([P, TILES, 1], F32, name="std")
             neg_mean = stat_pool.tile([P, TILES, 1], F32, name="neg_mean")
             nc.scalar.activation(
-                out=std[:], in_=stats[u]["mean_var"][:, :, 1:2], func=ACT.Sqrt, bias=eps[:], scale=1.0
+                out=std[:, :tiles],
+                in_=stats[u]["mean_var"][:, :tiles, 1:2],
+                func=ACT.Sqrt,
+                bias=eps[:],
+                scale=1.0,
             )
-            nc.scalar.mul(out=neg_mean[:], in_=stats[u]["mean_var"][:, :, 0:1], mul=-1.0)
+            nc.scalar.mul(
+                out=neg_mean[:, :tiles], in_=stats[u]["mean_var"][:, :tiles, 0:1], mul=-1.0
+            )
             stats[u]["std"] = std
             stats[u]["neg_mean"] = neg_mean
 
         def reciprocal_std(u):
             rstd = stat_pool.tile([P, TILES, 1], F32, name="rstd")
-            nc.vector.reciprocal(out=rstd[:], in_=stats[u]["std"][:])
+            tiles = units[u][2]
+            nc.vector.reciprocal(out=rstd[:, :tiles], in_=stats[u]["std"][:, :tiles])
             stats[u]["rstd"] = rstd
 
         def normalise(u):
             x_sb = x_tiles[u]
             s = stats[u]
             z = z_pool.tile([P, TILES, PASSES, PACK, P], F32, name="z")
-            for j in range(TILES):
+            for j in range(units[u][2]):
                 nc.gpsimd.tensor_scalar(
                     out=z[:, j],
                     in0=x_sb[:, j, :].rearrange("r (g p t) -> r g t p", g=PASSES, t=PACK),
@@ -164,18 +182,19 @@ def tile_vit_transformerblock_pa_t_kernel(
 
         def transpose_and_scale(u):
             z = z_tiles[u]
+            tiles = units[u][2]
             planes = h_pool.tile([P, PASSES, PACK, UNIT], BF16, name="planes", bufs=AHEAD - 1)
             for g in reversed(range(PASSES)):
                 for t in range(PACK):
                     zt = zt_pool.tile([P, UNIT], F32, name="zt")
-                    for j in range(TILES):
+                    for j in range(tiles):
                         nc.tensor.transpose(
                             out=zt[:, j * P : (j + 1) * P], in_=z[:, j, g, t, :], identity=identity[:]
                         )
                     plane = g * PACK + t
                     nc.scalar.activation(
-                        out=planes[:, g, t, :],
-                        in_=zt[:],
+                        out=planes[:, g, t, : tiles * P],
+                        in_=zt[:, : tiles * P],
                         func=ACT.Identity,
                         scale=affine[:, 0, plane : plane + 1],
                         bias=affine[:, 1, plane : plane + 1],
@@ -190,33 +209,40 @@ def tile_vit_transformerblock_pa_t_kernel(
                 in_=h_tiles[u]["planes"][:, g, :, first:last].rearrange("p t (c i) -> p c t i", i=RUN),
             )
 
+        def by_pass(tile_ap, u, per_row):
+            width = units[u][2] * P * per_row
+            return tile_ap[:, : PASSES * width].rearrange("p (g e) -> p g e", g=PASSES)
+
         def regroup_on_scalar(u):
-            h_tiles[u]["grouped"] = h_pool.tile(
-                [P, PASSES, UNIT * PACK], BF16, name="grouped", align_bytes=64, bufs=AHEAD
+            rows = units[u][2] * P
+            grouped = h_pool.tile(
+                [P, PASSES * UNIT * PACK], BF16, name="grouped", align_bytes=64, bufs=AHEAD
             )
-            regroup(nc.scalar.copy, u, 1, 0, UNIT)
-            regroup(nc.scalar.copy, u, 0, VECTOR_COLUMNS, UNIT)
+            h_tiles[u]["grouped"] = by_pass(grouped, u, PACK)
+            regroup(nc.scalar.copy, u, 1, 0, rows)
+            regroup(nc.scalar.copy, u, 0, VECTOR_COLUMNS * rows // UNIT, rows)
 
         def regroup_on_vector(u):
-            regroup(nc.vector.tensor_copy, u, 0, 0, VECTOR_COLUMNS)
+            rows = units[u][2] * P
+            regroup(nc.vector.tensor_copy, u, 0, 0, VECTOR_COLUMNS * rows // UNIT)
 
         def quantise(u):
-            codes = h_pool.tile([P, PASSES, UNIT], U32, name="codes", align_bytes=64)
-            scales = h_pool.tile([P, PASSES, UNIT], U8, name="scales", align_bytes=64)
+            codes = h_pool.tile([P, PASSES * UNIT], U32, name="codes", align_bytes=64)
+            scales = h_pool.tile([P, PASSES * UNIT], U8, name="scales", align_bytes=64)
+            h_tiles[u]["codes"] = by_pass(codes, u, 1)
+            h_tiles[u]["scales"] = by_pass(scales, u, 1)
             nc.vector.quantize_mx(
-                out=codes[:].rearrange("p g c -> p (g c)").bitcast(FP8X4),
-                scales=scales[:].rearrange("p g c -> p (g c)"),
-                in_=h_tiles[u]["grouped"][:].rearrange("p g e -> p (g e)"),
+                out=h_tiles[u]["codes"].rearrange("p g c -> p (g c)").bitcast(FP8X4),
+                scales=h_tiles[u]["scales"].rearrange("p g c -> p (g c)"),
+                in_=h_tiles[u]["grouped"].rearrange("p g e -> p (g e)"),
             )
-            h_tiles[u]["codes"] = codes
-            h_tiles[u]["scales"] = scales
 
         def project(u):
             h = h_tiles[u]
             acc_tiles[u] = []
             for w in range(3):
                 acc = acc_pool.tile([P, TILES, E], F32, name="acc%d" % w)
-                for j in range(TILES):
+                for j in range(units[u][2]):
                     rows = slice(j * P, (j + 1) * P)
                     for g in range(PASSES):
                         nc.tensor.matmul_mx(
@@ -231,16 +257,22 @@ def tile_vit_transformerblock_pa_t_kernel(
                 acc_tiles[u].append(acc)
 
         def finish(u):
-            result = o_pool.tile([P, 3, HEADS, TILES, HEAD_DIM], F32, name="result")
+            block, first, tiles = units[u]
+            result_tile = o_pool.tile([P, 3 * HEADS * TILES * HEAD_DIM], F32, name="result")
+            result = result_tile[:, : 3 * HEADS * tiles * HEAD_DIM].rearrange(
+                "p (w a j d) -> p w a j d", w=3, a=HEADS, j=tiles
+            )
             for w, acc in enumerate(acc_tiles[u]):
                 nc.vector.tensor_tensor(
                     out=result[:, w].rearrange("p a j d -> p j a d"),
-                    in0=acc[:].rearrange("p j (a d) -> p j a d", a=HEADS),
-                    in1=bias[:, w].to_broadcast([P, TILES, HEADS, HEAD_DIM]),
+                    in0=acc[:, :tiles].rearrange("p j (a d) -> p j a d", a=HEADS),
+                    in1=bias[:, w].to_broadcast([P, tiles, HEADS, HEAD_DIM]),
                     op=ALU.add,
                 )
                 nc.sync.dma_start(
-                    out=out_units[w][u // UNITS_PER_BATCH, u % UNITS_PER_BATCH],
+                    out=out_units[w][block // BLOCKS_PER_BATCH, block % BLOCKS_PER_BATCH][
+                        :, :, first * HEAD_DIM : (first + tiles) * HEAD_DIM
+                    ],
                     in_=result[:, w].rearrange("p a j d -> p a (j d)"),
                 )
 

@@ -86,44 +86,58 @@ def tile_vit_transformerblock_pa_t_kernel(
                 nc.sync.dma_start(out=x_sb[:, j, :], in_=x_units[block][:, first + j, :])
             x_tiles[u] = x_sb
 
-        def load_constants():
-            identity = const.tile([P, P], F32, name="identity")
-            make_identity(nc, identity[:])
-            eps = const.tile([P, 1], F32, name="eps")
-            nc.vector.memset(eps[:], EPS)
+        identity = const.tile([P, P], F32, name="identity")
+        eps = const.tile([P, 1], F32, name="eps")
+        affine = const.tile([P, 2, PLANES], F32, name="affine")
+        affine_bf = [const.tile([P, PASSES, PACK], BF16, name="vec_bf%d" % i) for i in range(2)]
+        ones = const.tile([P, P], BF16, name="ones")
+        bias_rows = const.tile([P, 3, E], BF16, name="bias_rows")
+        bias = const.tile([P, 3, 1, HEADS, HEAD_DIM], F32, name="bias")
+        w_codes = const.tile([P, 3, PASSES, E], U32, name="w_codes", align_bytes=64)
+        w_scales = const.tile([P, 3, PASSES, E], U8, name="w_scales", align_bytes=64)
 
-            affine = const.tile([P, 2, PLANES], F32, name="affine")
-            for i, vec in enumerate((gamma, beta)):
-                vec_bf = const.tile([P, PASSES, PACK], BF16, name="vec_bf%d" % i)
+        def start_constants():
+            make_identity(nc, identity[:])
+            nc.vector.memset(eps[:], EPS)
+            nc.vector.memset(w_scales[:].rearrange("p w g n -> p (w g n)").bitcast(I32), 0)
+            nc.vector.memset(ones[:], 1.0)
+            nc.vector.memset(bias_rows[:], 0.0)
+            for vec_bf, vec in zip(affine_bf, (gamma, beta)):
                 nc.scalar.dma_start(
                     out=vec_bf[:], in_=vec.rearrange("(g p t) -> p g t", g=PASSES, p=P)
                 )
+            for w, b in enumerate((bq, bk, bv)):
+                nc.scalar.dma_start(
+                    out=bias_rows[0:1, w, :], in_=b.rearrange("(o e) -> o e", o=1)
+                )
+            spread = acc_pool.tile([P, TILES, E], F32, name="acc0")
+            nc.tensor.matmul(
+                out=spread[:, 0:3, :].rearrange("p w e -> p (w e)"),
+                lhsT=ones[:],
+                rhs=bias_rows[:].rearrange("p w e -> p (w e)"),
+                start=True,
+                stop=True,
+            )
+            return spread
+
+        def finish_constants(spread):
+            for i, vec_bf in enumerate(affine_bf):
                 nc.vector.tensor_copy(
                     out=affine[:, i, :], in_=vec_bf[:].rearrange("p g t -> p (g t)")
                 )
-
-            bias_bf = const.tile([P, 3, E], BF16, name="bias_bf")
-            for w, b in enumerate((bq, bk, bv)):
-                nc.scalar.dma_start(out=bias_bf[:, w, :], in_=b.partition_broadcast(P))
-            bias = const.tile([P, 3, 1, HEADS, HEAD_DIM], F32, name="bias")
             nc.vector.tensor_copy(
-                out=bias[:].rearrange("p w o a d -> p w (o a d)"), in_=bias_bf[:]
+                out=bias[:].rearrange("p w o a d -> p w (o a d)"), in_=spread[:, 0:3, :]
             )
 
-            w_codes = const.tile([P, 3, PASSES, E], U32, name="w_codes", align_bytes=64)
-            w_scales = const.tile([P, 3, PASSES, E], U8, name="w_scales", align_bytes=64)
-            nc.vector.memset(w_scales[:].rearrange("p w g n -> p (w g n)").bitcast(I32), 0)
-            for w, (words, scales) in enumerate(weights):
-                nc.sync.dma_start(
-                    out=w_codes[:, w].bitcast(I32),
-                    in_=words.rearrange("g p n t -> p g (n t)").bitcast(I32),
-                )
-                rows = scales.rearrange("g (Q r) n -> r Q g n", r=4)
-                for r in range(4):
-                    nc.sync.dma_start(
-                        out=w_scales[r:P:32, w].bitcast(I32), in_=rows[r].bitcast(I32)
-                    )
-            return identity, eps, affine, bias, w_codes, w_scales
+        def load_weight(w):
+            words, scales = weights[w]
+            nc.sync.dma_start(
+                out=w_codes[:, w].bitcast(I32),
+                in_=words.rearrange("g p n t -> p g (n t)").bitcast(I32),
+            )
+            rows = scales.rearrange("g (Q r) n -> r Q g n", r=4)
+            for r in range(4):
+                nc.sync.dma_start(out=w_scales[r:P:32, w].bitcast(I32), in_=rows[r].bitcast(I32))
 
         def row_statistics(u):
             x_sb = x_tiles[u]
@@ -283,15 +297,19 @@ def tile_vit_transformerblock_pa_t_kernel(
         with tc.manual_schedule():
             load(0)
             load(1)
-            identity, eps, affine, bias, w_codes, w_scales = load_constants()
+            spread = start_constants()
             for s in range(UNITS + AHEAD + 2):
                 run(load, s + 2)
+                if s < len(weights):
+                    load_weight(s)
                 run(quantise, s - AHEAD - 1)
                 run(regroup_on_vector, s - AHEAD)
                 run(reciprocal_std, s - 1)
                 run(normalise, s - 1)
                 run(finish, s - AHEAD - 2)
                 run(row_statistics, s)
+                if s == 0:
+                    finish_constants(spread)
                 run(transpose_and_scale, s - 2)
                 run(row_scalars, s)
                 run(regroup_on_scalar, s - 2)

@@ -103,7 +103,7 @@ def tile_vit_transformerblock_pa_t_kernel(
             nc.vector.memset(ones[:], 1.0)
             nc.vector.memset(bias_rows[:], 0.0)
             for vec_bf, vec in zip(affine_bf, (gamma, beta)):
-                nc.scalar.dma_start(
+                nc.sync.dma_start(
                     out=vec_bf[:], in_=vec.rearrange("(g p t) -> p g t", g=PASSES, p=P)
                 )
             for w, b in enumerate((bq, bk, bv)):

@@ -28,6 +28,7 @@ BLOCKS_PER_BATCH = SEQ // UNIT
 FINE_BLOCKS = 2
 BN_CHUNK = 512
 RUN = 4
+VECTOR_RUN = 8
 VECTOR_COLUMNS = 256
 AHEAD = 4
 
@@ -215,12 +216,14 @@ def tile_vit_transformerblock_pa_t_kernel(
                     )
             h_tiles[u] = {"planes": planes}
 
-        def regroup(copy, u, g, first, last):
+        def regroup(copy, u, g, first, last, run_length=RUN):
             copy(
                 out=h_tiles[u]["grouped"][:, g, first * PACK : last * PACK].rearrange(
-                    "p (c i t) -> p c t i", i=RUN, t=PACK
+                    "p (c i t) -> p c t i", i=run_length, t=PACK
                 ),
-                in_=h_tiles[u]["planes"][:, g, :, first:last].rearrange("p t (c i) -> p c t i", i=RUN),
+                in_=h_tiles[u]["planes"][:, g, :, first:last].rearrange(
+                    "p t (c i) -> p c t i", i=run_length
+                ),
             )
 
         def by_pass(tile_ap, u, per_row):
@@ -238,7 +241,7 @@ def tile_vit_transformerblock_pa_t_kernel(
 
         def regroup_on_vector(u):
             rows = units[u][2] * P
-            regroup(nc.vector.tensor_copy, u, 0, 0, VECTOR_COLUMNS * rows // UNIT)
+            regroup(nc.vector.tensor_copy, u, 0, 0, VECTOR_COLUMNS * rows // UNIT, VECTOR_RUN)
 
         def quantise(u):
             codes = h_pool.tile([P, PASSES * UNIT], U32, name="codes", align_bytes=64)

@@ -75,7 +75,8 @@ def tile_vit_transformerblock_pa_t_kernel(
         z_pool = ctx.enter_context(tc.tile_pool(name="z", bufs=2))
         h_pool = ctx.enter_context(tc.tile_pool(name="h", bufs=2))
         o_pool = ctx.enter_context(tc.tile_pool(name="o", bufs=2))
-        zt_pool = ctx.enter_context(tc.psum_pool(name="zt", bufs=5))
+        zt_pool = ctx.enter_context(tc.psum_pool(name="zt", bufs=4))
+        mix_pool = ctx.enter_context(tc.psum_pool(name="mix", bufs=1))
         acc_pool = ctx.enter_context(tc.psum_pool(name="acc", bufs=1))
 
         x_tiles, stats, z_tiles, h_tiles, acc_tiles = {}, {}, {}, {}, {}
@@ -88,6 +89,7 @@ def tile_vit_transformerblock_pa_t_kernel(
             x_tiles[u] = x_sb
 
         identity = const.tile([P, P], F32, name="identity")
+        identity_bf = const.tile([P, P], BF16, name="identity_bf")
         eps = const.tile([P, 1], F32, name="eps")
         affine = const.tile([P, 2, PLANES], F32, name="affine")
         affine_bf = [const.tile([P, PASSES, PACK], BF16, name="vec_bf%d" % i) for i in range(2)]
@@ -99,6 +101,7 @@ def tile_vit_transformerblock_pa_t_kernel(
 
         def start_constants():
             make_identity(nc, identity[:])
+            make_identity(nc, identity_bf[:])
             nc.vector.memset(eps[:], EPS)
             nc.vector.memset(w_scales[:].rearrange("p w g n -> p (w g n)").bitcast(I32), 0)
             nc.vector.memset(ones[:], 1.0)
@@ -237,7 +240,27 @@ def tile_vit_transformerblock_pa_t_kernel(
             )
             h_tiles[u]["grouped"] = by_pass(grouped, u, PACK)
             regroup(nc.scalar.copy, u, 1, 0, rows)
-            regroup(nc.scalar.copy, u, 0, VECTOR_COLUMNS * rows // UNIT, rows)
+
+        def regroup_on_tensor(u):
+            tiles = units[u][2]
+            vector_tiles = VECTOR_COLUMNS * tiles // UNIT
+            count = tiles - vector_tiles
+            mix = mix_pool.tile([P, TILES // 2, P, PACK], BF16, name="mix")
+            for i in range(count):
+                j = vector_tiles + i
+                nc.tensor.matmul(
+                    out=mix[:, i],
+                    lhsT=identity_bf[:],
+                    rhs=h_tiles[u]["planes"][:, 0, :, j * P : (j + 1) * P].rearrange(
+                        "p t c -> p c t"
+                    ),
+                    start=True,
+                    stop=True,
+                )
+            nc.scalar.copy(
+                out=h_tiles[u]["grouped"][:, 0, vector_tiles * P * PACK : tiles * P * PACK],
+                in_=mix[:, :count].rearrange("p i c t -> p (i c t)"),
+            )
 
         def regroup_on_vector(u):
             rows = units[u][2] * P
@@ -313,6 +336,7 @@ def tile_vit_transformerblock_pa_t_kernel(
                 run(row_statistics, s)
                 if s == 0:
                     finish_constants(spread)
+                run(regroup_on_tensor, s - 3)
                 run(transpose_and_scale, s - 2)
                 run(row_scalars, s)
                 run(regroup_on_scalar, s - 2)

@@ -29,6 +29,7 @@ FINE_BLOCKS = 2
 BN_CHUNK = 512
 RUN = 4
 VECTOR_RUN = 8
+TENSOR_RUN = 8
 VECTOR_COLUMNS = 256
 AHEAD = 4
 
@@ -249,10 +250,10 @@ def tile_vit_transformerblock_pa_t_kernel(
             for i in range(count):
                 j = vector_tiles + i
                 nc.tensor.matmul(
-                    out=mix[:, i],
+                    out=mix[:, i].rearrange("p (c i) t -> p c t i", i=TENSOR_RUN),
                     lhsT=identity_bf[:],
                     rhs=h_tiles[u]["planes"][:, 0, :, j * P : (j + 1) * P].rearrange(
-                        "p t c -> p c t"
+                        "p t (c i) -> p c t i", i=TENSOR_RUN
                     ),
                     start=True,
                     stop=True,

@@ -199,26 +199,27 @@ def tile_vit_transformerblock_pa_t_kernel(
                 )
             z_tiles[u] = z
 
-        def transpose_and_scale(u):
+        def transpose_and_scale(u, g):
             z = z_tiles[u]
             tiles = units[u][2]
-            planes = h_pool.tile([P, PASSES, PACK, UNIT], BF16, name="planes", bufs=AHEAD - 1)
-            for g in reversed(range(PASSES)):
-                for t in range(PACK):
-                    zt = zt_pool.tile([P, UNIT], F32, name="zt")
-                    for j in range(tiles):
-                        nc.tensor.transpose(
-                            out=zt[:, j * P : (j + 1) * P], in_=z[:, j, g, t, :], identity=identity[:]
-                        )
-                    plane = g * PACK + t
-                    nc.scalar.activation(
-                        out=planes[:, g, t, : tiles * P],
-                        in_=zt[:, : tiles * P],
-                        func=ACT.Identity,
-                        scale=affine[:, 0, plane : plane + 1],
-                        bias=affine[:, 1, plane : plane + 1],
+            if u not in h_tiles:
+                planes = h_pool.tile([P, PASSES, PACK, UNIT], BF16, name="planes", bufs=AHEAD - 1)
+                h_tiles[u] = {"planes": planes}
+            planes = h_tiles[u]["planes"]
+            for t in range(PACK):
+                zt = zt_pool.tile([P, UNIT], F32, name="zt")
+                for j in range(tiles):
+                    nc.tensor.transpose(
+                        out=zt[:, j * P : (j + 1) * P], in_=z[:, j, g, t, :], identity=identity[:]
                     )
-            h_tiles[u] = {"planes": planes}
+                plane = g * PACK + t
+                nc.scalar.activation(
+                    out=planes[:, g, t, : tiles * P],
+                    in_=zt[:, : tiles * P],
+                    func=ACT.Identity,
+                    scale=affine[:, 0, plane : plane + 1],
+                    bias=affine[:, 1, plane : plane + 1],
+                )
 
         def regroup(copy, u, g, first, last, run_length=RUN):
             copy(
@@ -317,9 +318,9 @@ def tile_vit_transformerblock_pa_t_kernel(
                     in_=result[:, w].rearrange("p a j d -> p a (j d)"),
                 )
 
-        def run(stage, u):
+        def run(stage, u, *rest):
             if 0 <= u < UNITS:
-                stage(u)
+                stage(u, *rest)
 
         with tc.manual_schedule():
             load(0)
@@ -337,8 +338,9 @@ def tile_vit_transformerblock_pa_t_kernel(
                 run(row_statistics, s)
                 if s == 0:
                     finish_constants(spread)
+                run(transpose_and_scale, s - 2, 1)
                 run(regroup_on_tensor, s - 3)
-                run(transpose_and_scale, s - 2)
+                run(transpose_and_scale, s - 2, 0)
                 run(row_scalars, s)
                 run(regroup_on_scalar, s - 2)
                 run(project, s - AHEAD - 1)

@@ -30,7 +30,8 @@ BN_CHUNK = 512
 RUN = 4
 VECTOR_RUN = 8
 TENSOR_RUN = 8
-VECTOR_COLUMNS = 256
+VECTOR_COLUMNS = 192
+TENSOR_COLUMNS = 256
 AHEAD = 4
 
 FLOPS = 2 * BATCH * SEQ * D * 3 * E
@@ -75,7 +76,7 @@ def tile_vit_transformerblock_pa_t_kernel(
         stat_pool = ctx.enter_context(tc.tile_pool(name="stat", bufs=4))
         z_pool = ctx.enter_context(tc.tile_pool(name="z", bufs=2))
         h_pool = ctx.enter_context(tc.tile_pool(name="h", bufs=2))
-        o_pool = ctx.enter_context(tc.tile_pool(name="o", bufs=2))
+        o_pool = ctx.enter_context(tc.tile_pool(name="o", bufs=4))
         zt_pool = ctx.enter_context(tc.psum_pool(name="zt", bufs=4))
         mix_pool = ctx.enter_context(tc.psum_pool(name="mix", bufs=1))
         acc_pool = ctx.enter_context(tc.psum_pool(name="acc", bufs=1))
@@ -242,14 +243,21 @@ def tile_vit_transformerblock_pa_t_kernel(
             )
             h_tiles[u]["grouped"] = by_pass(grouped, u, PACK)
             regroup(nc.scalar.copy, u, 1, 0, rows)
+            regroup(
+                nc.scalar.copy,
+                u,
+                0,
+                VECTOR_COLUMNS * rows // UNIT,
+                (UNIT - TENSOR_COLUMNS) * rows // UNIT,
+            )
 
         def regroup_on_tensor(u):
             tiles = units[u][2]
-            vector_tiles = VECTOR_COLUMNS * tiles // UNIT
-            count = tiles - vector_tiles
+            count = TENSOR_COLUMNS * tiles // UNIT
+            first_tile = tiles - count
             mix = mix_pool.tile([P, TILES // 2, P, PACK], BF16, name="mix")
             for i in range(count):
-                j = vector_tiles + i
+                j = first_tile + i
                 nc.tensor.matmul(
                     out=mix[:, i].rearrange("p (c i) t -> p c t i", i=TENSOR_RUN),
                     lhsT=identity_bf[:],
@@ -260,7 +268,7 @@ def tile_vit_transformerblock_pa_t_kernel(
                     stop=True,
                 )
             nc.scalar.copy(
-                out=h_tiles[u]["grouped"][:, 0, vector_tiles * P * PACK : tiles * P * PACK],
+                out=h_tiles[u]["grouped"][:, 0, first_tile * P * PACK : tiles * P * PACK],
                 in_=mix[:, :count].rearrange("p i c t -> p (i c t)"),
             )
 

@@ -25,7 +25,7 @@ TILES = 4
 UNIT = P * TILES
 BLOCKS = BATCH * SEQ // UNIT
 BLOCKS_PER_BATCH = SEQ // UNIT
-FINE_BLOCKS = 2
+FINE_FIRST, FINE_LAST = 1, 2
 BN_CHUNK = 512
 RUN = 4
 VECTOR_RUN = 8
@@ -64,7 +64,7 @@ def tile_vit_transformerblock_pa_t_kernel(
     ]
     units = []
     for block in range(BLOCKS):
-        if block < FINE_BLOCKS or block >= BLOCKS - FINE_BLOCKS:
+        if block < FINE_FIRST or block >= BLOCKS - FINE_LAST:
             units.extend([(block, 0, TILES // 2), (block, TILES // 2, TILES // 2)])
         else:
             units.append((block, 0, TILES))

@@ -69,6 +69,7 @@ def tile_vit_transformerblock_pa_t_kernel(
         else:
             units.append((block, 0, TILES))
     UNITS = len(units)
+    FIRST_WHOLE = 2 * FINE_FIRST
 
     with ExitStack() as ctx:
         const = ctx.enter_context(tc.tile_pool(name="const", bufs=1))
@@ -126,11 +127,13 @@ def tile_vit_transformerblock_pa_t_kernel(
             )
             return spread
 
-        def finish_constants(spread):
+        def cast_affine():
             for i, vec_bf in enumerate(affine_bf):
                 nc.vector.tensor_copy(
                     out=affine[:, i, :], in_=vec_bf[:].rearrange("p g t -> p (g t)")
                 )
+
+        def cast_bias(spread):
             nc.vector.tensor_copy(
                 out=bias[:].rearrange("p w o a d -> p w (o a d)"), in_=spread[:, 0:3, :]
             )
@@ -164,35 +167,56 @@ def tile_vit_transformerblock_pa_t_kernel(
 
         def row_scalars(u):
             tiles = units[u][2]
-            std = stat_pool.tile([P, TILES, 1], F32, name="std")
-            neg_mean = stat_pool.tile([P, TILES, 1], F32, name="neg_mean")
+            rstd = stat_pool.tile([P, TILES, 1], F32, name="rstd")
             nc.scalar.activation(
-                out=std[:, :tiles],
+                out=rstd[:, :tiles],
                 in_=stats[u]["mean_var"][:, :tiles, 1:2],
-                func=ACT.Sqrt,
+                func=ACT.Abs_reciprocal_sqrt,
                 bias=eps[:],
                 scale=1.0,
             )
-            nc.scalar.mul(
-                out=neg_mean[:, :tiles], in_=stats[u]["mean_var"][:, :tiles, 0:1], mul=-1.0
+            stats[u]["rstd"] = rstd
+
+        def negate_mean(u):
+            tiles = units[u][2]
+            neg_mean = stat_pool.tile([P, TILES, 1], F32, name="neg_mean")
+            nc.vector.tensor_scalar(
+                out=neg_mean[:, :tiles],
+                in0=stats[u]["mean_var"][:, :tiles, 0:1],
+                scalar1=-1.0,
+                scalar2=None,
+                op0=ALU.mult,
             )
-            stats[u]["std"] = std
             stats[u]["neg_mean"] = neg_mean
 
-        def reciprocal_std(u):
-            rstd = stat_pool.tile([P, TILES, 1], F32, name="rstd")
-            tiles = units[u][2]
-            nc.vector.reciprocal(out=rstd[:, :tiles], in_=stats[u]["std"][:, :tiles])
-            stats[u]["rstd"] = rstd
+        def by_block(x_row):
+            return x_row.rearrange("r (g p t) -> r g t p", g=PASSES, t=PACK)
+
+        def normalise_on_scalar(u):
+            if u != FIRST_WHOLE:
+                return
+            s = stats[u]
+            j = units[u][2] - 1
+            shift = stat_pool.tile([P, 1], F32, name="shift", bufs=1)
+            nc.scalar.activation(
+                out=shift[:], in_=s["neg_mean"][:, j, :], func=ACT.Copy, scale=s["rstd"][:, j, :]
+            )
+            nc.scalar.activation(
+                out=z_tiles[u][:, j],
+                in_=by_block(x_tiles[u][:, j, :]),
+                func=ACT.Identity,
+                scale=s["rstd"][:, j, :],
+                bias=shift[:],
+            )
 
         def normalise(u):
             x_sb = x_tiles[u]
             s = stats[u]
             z = z_pool.tile([P, TILES, PASSES, PACK, P], F32, name="z")
-            for j in range(units[u][2]):
+            for j in range(units[u][2] - (u == FIRST_WHOLE)):
                 nc.gpsimd.tensor_scalar(
                     out=z[:, j],
-                    in0=x_sb[:, j, :].rearrange("r (g p t) -> r g t p", g=PASSES, t=PACK),
+                    in0=by_block(x_sb[:, j, :]),
                     scalar1=s["neg_mean"][:, j, :],
                     scalar2=s["rstd"][:, j, :],
                     op0=ALU.add,
@@ -340,14 +364,17 @@ def tile_vit_transformerblock_pa_t_kernel(
                     load_weight(s)
                 run(quantise, s - AHEAD - 1)
                 run(regroup_on_vector, s - AHEAD)
-                run(reciprocal_std, s - 1)
+                run(negate_mean, s - 1)
                 run(normalise, s - 1)
                 run(finish, s - AHEAD - 2)
+                if s == 1:
+                    cast_affine()
+                if s == AHEAD:
+                    cast_bias(spread)
                 run(row_statistics, s)
-                if s == 0:
-                    finish_constants(spread)
                 run(transpose_and_scale, s - 2, 1)
                 run(regroup_on_tensor, s - 3)
+                run(normalise_on_scalar, s - 1)
                 run(transpose_and_scale, s - 2, 0)
                 run(row_scalars, s)
                 run(regroup_on_scalar, s - 2)

@@ -25,13 +25,14 @@ TILES = 4
 UNIT = P * TILES
 BLOCKS = BATCH * SEQ // UNIT
 BLOCKS_PER_BATCH = SEQ // UNIT
-FINE_FIRST, FINE_LAST = 1, 2
+FINE = 3
 BN_CHUNK = 512
 RUN = 4
 VECTOR_RUN = 8
 TENSOR_RUN = 8
-VECTOR_COLUMNS = 192
+VECTOR_COLUMNS = 160
 TENSOR_COLUMNS = 256
+LATE = 6
 AHEAD = 4
 
 FLOPS = 2 * BATCH * SEQ * D * 3 * E
@@ -62,14 +63,11 @@ def tile_vit_transformerblock_pa_t_kernel(
         o.rearrange("b a (h p j) d -> b h p a (j d)", h=BLOCKS_PER_BATCH, p=P, j=TILES)
         for o in (out_0, out_1, out_2)
     ]
-    units = []
-    for block in range(BLOCKS):
-        if block < FINE_FIRST or block >= BLOCKS - FINE_LAST:
-            units.extend([(block, 0, TILES // 2), (block, TILES // 2, TILES // 2)])
-        else:
-            units.append((block, 0, TILES))
+    halves = [(b, j, TILES // 2) for b in (0, 1, BLOCKS - 1) for j in (0, TILES // 2)]
+    whole = [(b, 0, TILES) for b in range(2, BLOCKS - 1)]
+    units = halves[:FINE] + whole + halves[FINE:]
     UNITS = len(units)
-    FIRST_WHOLE = 2 * FINE_FIRST
+    FIRST_WHOLE = FINE
 
     with ExitStack() as ctx:
         const = ctx.enter_context(tc.tile_pool(name="const", bufs=1))
@@ -246,6 +244,10 @@ def tile_vit_transformerblock_pa_t_kernel(
                     bias=affine[:, 1, plane : plane + 1],
                 )
 
+        def vector_columns(u):
+            columns = VECTOR_COLUMNS if u < UNITS - LATE else UNIT - TENSOR_COLUMNS
+            return columns * units[u][2] // TILES
+
         def regroup(copy, u, g, first, last, run_length=RUN):
             copy(
                 out=h_tiles[u]["grouped"][:, g, first * PACK : last * PACK].rearrange(
@@ -267,13 +269,9 @@ def tile_vit_transformerblock_pa_t_kernel(
             )
             h_tiles[u]["grouped"] = by_pass(grouped, u, PACK)
             regroup(nc.scalar.copy, u, 1, 0, rows)
-            regroup(
-                nc.scalar.copy,
-                u,
-                0,
-                VECTOR_COLUMNS * rows // UNIT,
-                (UNIT - TENSOR_COLUMNS) * rows // UNIT,
-            )
+            tensor_first = (UNIT - TENSOR_COLUMNS) * rows // UNIT
+            if vector_columns(u) < tensor_first:
+                regroup(nc.scalar.copy, u, 0, vector_columns(u), tensor_first)
 
         def regroup_on_tensor(u):
             tiles = units[u][2]
@@ -297,8 +295,7 @@ def tile_vit_transformerblock_pa_t_kernel(
             )
 
         def regroup_on_vector(u):
-            rows = units[u][2] * P
-            regroup(nc.vector.tensor_copy, u, 0, 0, VECTOR_COLUMNS * rows // UNIT, VECTOR_RUN)
+            regroup(nc.vector.tensor_copy, u, 0, 0, vector_columns(u), VECTOR_RUN)
 
         def quantise(u):
             codes = h_pool.tile([P, PASSES * UNIT], U32, name="codes", align_bytes=64)

@@ -68,6 +68,7 @@ def tile_vit_transformerblock_pa_t_kernel(
     units = halves[:FINE] + whole + halves[FINE:]
     UNITS = len(units)
     FIRST_WHOLE = FINE
+    LAST = UNITS - 1
 
     with ExitStack() as ctx:
         const = ctx.enter_context(tc.tile_pool(name="const", bufs=1))
@@ -245,6 +246,8 @@ def tile_vit_transformerblock_pa_t_kernel(
                 )
 
         def vector_columns(u):
+            if u == LAST:
+                return 0
             columns = VECTOR_COLUMNS if u < UNITS - LATE else UNIT - TENSOR_COLUMNS
             return columns * units[u][2] // TILES
 
@@ -295,7 +298,8 @@ def tile_vit_transformerblock_pa_t_kernel(
             )
 
         def regroup_on_vector(u):
-            regroup(nc.vector.tensor_copy, u, 0, 0, vector_columns(u), VECTOR_RUN)
+            if u != LAST:
+                regroup(nc.vector.tensor_copy, u, 0, 0, vector_columns(u), VECTOR_RUN)
 
         def quantise(u):
             codes = h_pool.tile([P, PASSES * UNIT], U32, name="codes", align_bytes=64)
@@ -312,7 +316,11 @@ def tile_vit_transformerblock_pa_t_kernel(
             h = h_tiles[u]
             acc_tiles[u] = []
             for w in range(3):
-                acc = acc_pool.tile([P, TILES, E], F32, name="acc%d" % w)
+                if u == LAST:
+                    bank = zt_pool.tile([P, UNIT], F32, name="zt")
+                    acc = bank[:].rearrange("p (j e) -> p j e", j=TILES)
+                else:
+                    acc = acc_pool.tile([P, TILES, E], F32, name="acc%d" % w)
                 for j in range(units[u][2]):
                     rows = slice(j * P, (j + 1) * P)
                     for g in range(PASSES):

@@ -67,7 +67,7 @@ def tile_vit_transformerblock_pa_t_kernel(
     whole = [(b, 0, TILES) for b in range(2, BLOCKS - 1)]
     units = halves[:FINE] + whole + halves[FINE:]
     UNITS = len(units)
-    FIRST_WHOLE = FINE
+    SHARED = (0, FINE)
     LAST = UNITS - 1
 
     with ExitStack() as ctx:
@@ -192,7 +192,7 @@ def tile_vit_transformerblock_pa_t_kernel(
             return x_row.rearrange("r (g p t) -> r g t p", g=PASSES, t=PACK)
 
         def normalise_on_scalar(u):
-            if u != FIRST_WHOLE:
+            if u not in SHARED:
                 return
             s = stats[u]
             j = units[u][2] - 1
@@ -212,7 +212,7 @@ def tile_vit_transformerblock_pa_t_kernel(
             x_sb = x_tiles[u]
             s = stats[u]
             z = z_pool.tile([P, TILES, PASSES, PACK, P], F32, name="z")
-            for j in range(units[u][2] - (u == FIRST_WHOLE)):
+            for j in range(units[u][2] - (u in SHARED)):
                 nc.gpsimd.tensor_scalar(
                     out=z[:, j],
                     in0=by_block(x_sb[:, j, :]),

from contextlib import ExitStack

import concourse.mybir as mybir
from concourse.masks import make_identity

F32 = mybir.dt.float32
BF16 = mybir.dt.bfloat16
I32 = mybir.dt.int32
U32 = mybir.dt.uint32
U8 = mybir.dt.uint8
FP8X4 = mybir.dt.float8_e4m3fn_x4
ALU = mybir.AluOpType
ACT = mybir.ActivationFunctionType

P = 128
BATCH, SEQ, D = 8, 1024, 1024
HEADS, HEAD_DIM = 2, 64
E = HEADS * HEAD_DIM
EPS = 1e-5
PACK = 4
K_PASS = P * PACK
PASSES = D // K_PASS
PLANES = PASSES * PACK
TILES = 4
UNIT = P * TILES
BLOCKS = BATCH * SEQ // UNIT
BLOCKS_PER_BATCH = SEQ // UNIT
FINE = 3
BN_CHUNK = 512
RUN = 4
VECTOR_RUN = 8
TENSOR_RUN = 8
VECTOR_COLUMNS = 160
TENSOR_COLUMNS = 256
LATE = 6
AHEAD = 4

FLOPS = 2 * BATCH * SEQ * D * 3 * E


def tile_vit_transformerblock_pa_t_kernel(
    tc,
    x,
    gamma,
    beta,
    Wq_words,
    Wq_scales,
    bq,
    Wk_words,
    Wk_scales,
    bk,
    Wv_words,
    Wv_scales,
    bv,
    out_0,
    out_1,
    out_2,
):
    nc = tc.nc
    weights = ((Wq_words, Wq_scales), (Wk_words, Wk_scales), (Wv_words, Wv_scales))
    x_units = x.flatten_outer_dims().rearrange("(u p j) k -> u p j k", p=P, j=TILES)
    out_units = [
        o.rearrange("b a (h p j) d -> b h p a (j d)", h=BLOCKS_PER_BATCH, p=P, j=TILES)
        for o in (out_0, out_1, out_2)
    ]
    halves = [(b, j, TILES // 2) for b in (0, 1, BLOCKS - 1) for j in (0, TILES // 2)]
    whole = [(b, 0, TILES) for b in range(2, BLOCKS - 1)]
    units = halves[:FINE] + whole + halves[FINE:]
    UNITS = len(units)
    SHARED = (0, FINE)
    LAST = UNITS - 1

    with ExitStack() as ctx:
        const = ctx.enter_context(tc.tile_pool(name="const", bufs=1))
        x_pool = ctx.enter_context(tc.tile_pool(name="x", bufs=AHEAD + 2))
        stat_pool = ctx.enter_context(tc.tile_pool(name="stat", bufs=4))
        z_pool = ctx.enter_context(tc.tile_pool(name="z", bufs=2))
        h_pool = ctx.enter_context(tc.tile_pool(name="h", bufs=2))
        o_pool = ctx.enter_context(tc.tile_pool(name="o", bufs=4))
        zt_pool = ctx.enter_context(tc.psum_pool(name="zt", bufs=4))
        mix_pool = ctx.enter_context(tc.psum_pool(name="mix", bufs=1))
        acc_pool = ctx.enter_context(tc.psum_pool(name="acc", bufs=1))

        x_tiles, stats, z_tiles, h_tiles, acc_tiles = {}, {}, {}, {}, {}

        def load(u):
            block, first, tiles = units[u]
            x_sb = x_pool.tile([P, TILES, D], BF16, name="x_sb")
            for j in range(tiles):
                nc.sync.dma_start(out=x_sb[:, j, :], in_=x_units[block][:, first + j, :])
            x_tiles[u] = x_sb

        identity = const.tile([P, P], F32, name="identity")
        identity_bf = const.tile([P, P], BF16, name="identity_bf")
        eps = const.tile([P, 1], F32, name="eps")
        affine = const.tile([P, 2, PLANES], F32, name="affine")
        affine_bf = [const.tile([P, PASSES, PACK], BF16, name="vec_bf%d" % i) for i in range(2)]
        ones = const.tile([P, P], BF16, name="ones")
        bias_rows = const.tile([P, 3, E], BF16, name="bias_rows")
        bias = const.tile([P, 3, 1, HEADS, HEAD_DIM], F32, name="bias")
        w_codes = const.tile([P, 3, PASSES, E], U32, name="w_codes", align_bytes=64)
        w_scales = const.tile([P, 3, PASSES, E], U8, name="w_scales", align_bytes=64)

        def start_constants():
            make_identity(nc, identity[:])
            make_identity(nc, identity_bf[:])
            nc.vector.memset(eps[:], EPS)
            nc.vector.memset(w_scales[:].rearrange("p w g n -> p (w g n)").bitcast(I32), 0)
            nc.vector.memset(ones[:], 1.0)
            nc.vector.memset(bias_rows[:], 0.0)
            for vec_bf, vec in zip(affine_bf, (gamma, beta)):
                nc.sync.dma_start(
                    out=vec_bf[:], in_=vec.rearrange("(g p t) -> p g t", g=PASSES, p=P)
                )
            for w, b in enumerate((bq, bk, bv)):
                nc.scalar.dma_start(
                    out=bias_rows[0:1, w, :], in_=b.rearrange("(o e) -> o e", o=1)
                )
            spread = acc_pool.tile([P, TILES, E], F32, name="acc0")
            nc.tensor.matmul(
                out=spread[:, 0:3, :].rearrange("p w e -> p (w e)"),
                lhsT=ones[:],
                rhs=bias_rows[:].rearrange("p w e -> p (w e)"),
                start=True,
                stop=True,
            )
            return spread

        def cast_affine():
            for i, vec_bf in enumerate(affine_bf):
                nc.vector.tensor_copy(
                    out=affine[:, i, :], in_=vec_bf[:].rearrange("p g t -> p (g t)")
                )

        def cast_bias(spread):
            nc.vector.tensor_copy(
                out=bias[:].rearrange("p w o a d -> p w (o a d)"), in_=spread[:, 0:3, :]
            )

        def load_weight(w):
            words, scales = weights[w]
            nc.sync.dma_start(
                out=w_codes[:, w].bitcast(I32),
                in_=words.rearrange("g p n t -> p g (n t)").bitcast(I32),
            )
            rows = scales.rearrange("g (Q r) n -> r Q g n", r=4)
            for r in range(4):
                nc.sync.dma_start(out=w_scales[r:P:32, w].bitcast(I32), in_=rows[r].bitcast(I32))

        def row_statistics(u):
            x_sb = x_tiles[u]
            tiles = units[u][2]
            chunks = D // BN_CHUNK
            partial = stat_pool.tile([P, TILES, chunks, 6], F32, name="partial")
            mean_var = stat_pool.tile([P, TILES, 2], F32, name="mean_var")
            for j in range(tiles):
                for c in range(chunks):
                    nc.vector.bn_stats(
                        out=partial[:, j, c, :], in_=x_sb[:, j, c * BN_CHUNK : (c + 1) * BN_CHUNK]
                    )
            for j in range(tiles):
                nc.vector.bn_aggr(
                    out=mean_var[:, j, :], in_=partial[:, j].rearrange("p c s -> p (c s)")
                )
            stats[u] = {"mean_var": mean_var}

        def row_scalars(u):
            tiles = units[u][2]
            rstd = stat_pool.tile([P, TILES, 1], F32, name="rstd")
            nc.scalar.activation(
                out=rstd[:, :tiles],
                in_=stats[u]["mean_var"][:, :tiles, 1:2],
                func=ACT.Abs_reciprocal_sqrt,
                bias=eps[:],
                scale=1.0,
            )
            stats[u]["rstd"] = rstd

        def negate_mean(u):
            tiles = units[u][2]
            neg_mean = stat_pool.tile([P, TILES, 1], F32, name="neg_mean")
            nc.vector.tensor_scalar(
                out=neg_mean[:, :tiles],
                in0=stats[u]["mean_var"][:, :tiles, 0:1],
                scalar1=-1.0,
                scalar2=None,
                op0=ALU.mult,
            )
            stats[u]["neg_mean"] = neg_mean

        def by_block(x_row):
            return x_row.rearrange("r (g p t) -> r g t p", g=PASSES, t=PACK)

        def normalise_on_scalar(u):
            if u not in SHARED:
                return
            s = stats[u]
            j = units[u][2] - 1
            shift = stat_pool.tile([P, 1], F32, name="shift", bufs=1)
            nc.scalar.activation(
                out=shift[:], in_=s["neg_mean"][:, j, :], func=ACT.Copy, scale=s["rstd"][:, j, :]
            )
            nc.scalar.activation(
                out=z_tiles[u][:, j],
                in_=by_block(x_tiles[u][:, j, :]),
                func=ACT.Identity,
                scale=s["rstd"][:, j, :],
                bias=shift[:],
            )

        def normalise(u):
            x_sb = x_tiles[u]
            s = stats[u]
            z = z_pool.tile([P, TILES, PASSES, PACK, P], F32, name="z")
            for j in range(units[u][2] - (u in SHARED)):
                nc.gpsimd.tensor_scalar(
                    out=z[:, j],
                    in0=by_block(x_sb[:, j, :]),
                    scalar1=s["neg_mean"][:, j, :],
                    scalar2=s["rstd"][:, j, :],
                    op0=ALU.add,
                    op1=ALU.mult,
                )
            z_tiles[u] = z

        def transpose_and_scale(u, g):
            z = z_tiles[u]
            tiles = units[u][2]
            if u not in h_tiles:
                planes = h_pool.tile([P, PASSES, PACK, UNIT], BF16, name="planes", bufs=AHEAD - 1)
                h_tiles[u] = {"planes": planes}
            planes = h_tiles[u]["planes"]
            for t in range(PACK):
                zt = zt_pool.tile([P, UNIT], F32, name="zt")
                for j in range(tiles):
                    nc.tensor.transpose(
                        out=zt[:, j * P : (j + 1) * P], in_=z[:, j, g, t, :], identity=identity[:]
                    )
                plane = g * PACK + t
                nc.scalar.activation(
                    out=planes[:, g, t, : tiles * P],
                    in_=zt[:, : tiles * P],
                    func=ACT.Identity,
                    scale=affine[:, 0, plane : plane + 1],
                    bias=affine[:, 1, plane : plane + 1],
                )

        def vector_columns(u):
            if u == LAST:
                return 0
            columns = VECTOR_COLUMNS if u < UNITS - LATE else UNIT - TENSOR_COLUMNS
            return columns * units[u][2] // TILES

        def regroup(copy, u, g, first, last, run_length=RUN):
            copy(
                out=h_tiles[u]["grouped"][:, g, first * PACK : last * PACK].rearrange(
                    "p (c i t) -> p c t i", i=run_length, t=PACK
                ),
                in_=h_tiles[u]["planes"][:, g, :, first:last].rearrange(
                    "p t (c i) -> p c t i", i=run_length
                ),
            )

        def by_pass(tile_ap, u, per_row):
            width = units[u][2] * P * per_row
            return tile_ap[:, : PASSES * width].rearrange("p (g e) -> p g e", g=PASSES)

        def regroup_on_scalar(u):
            rows = units[u][2] * P
            grouped = h_pool.tile(
                [P, PASSES * UNIT * PACK], BF16, name="grouped", align_bytes=64, bufs=AHEAD
            )
            h_tiles[u]["grouped"] = by_pass(grouped, u, PACK)
            regroup(nc.scalar.copy, u, 1, 0, rows)
            tensor_first = (UNIT - TENSOR_COLUMNS) * rows // UNIT
            if vector_columns(u) < tensor_first:
                regroup(nc.scalar.copy, u, 0, vector_columns(u), tensor_first)

        def regroup_on_tensor(u):
            tiles = units[u][2]
            count = TENSOR_COLUMNS * tiles // UNIT
            first_tile = tiles - count
            mix = mix_pool.tile([P, TILES // 2, P, PACK], BF16, name="mix")
            for i in range(count):
                j = first_tile + i
                nc.tensor.matmul(
                    out=mix[:, i].rearrange("p (c i) t -> p c t i", i=TENSOR_RUN),
                    lhsT=identity_bf[:],
                    rhs=h_tiles[u]["planes"][:, 0, :, j * P : (j + 1) * P].rearrange(
                        "p t (c i) -> p c t i", i=TENSOR_RUN
                    ),
                    start=True,
                    stop=True,
                )
            nc.scalar.copy(
                out=h_tiles[u]["grouped"][:, 0, first_tile * P * PACK : tiles * P * PACK],
                in_=mix[:, :count].rearrange("p i c t -> p (i c t)"),
            )

        def regroup_on_vector(u):
            if u != LAST:
                regroup(nc.vector.tensor_copy, u, 0, 0, vector_columns(u), VECTOR_RUN)

        def quantise(u):
            codes = h_pool.tile([P, PASSES * UNIT], U32, name="codes", align_bytes=64)
            scales = h_pool.tile([P, PASSES * UNIT], U8, name="scales", align_bytes=64)
            h_tiles[u]["codes"] = by_pass(codes, u, 1)
            h_tiles[u]["scales"] = by_pass(scales, u, 1)
            nc.vector.quantize_mx(
                out=h_tiles[u]["codes"].rearrange("p g c -> p (g c)").bitcast(FP8X4),
                scales=h_tiles[u]["scales"].rearrange("p g c -> p (g c)"),
                in_=h_tiles[u]["grouped"].rearrange("p g e -> p (g e)"),
            )

        def project(u):
            h = h_tiles[u]
            acc_tiles[u] = []
            for w in range(3):
                if u == LAST:
                    bank = zt_pool.tile([P, UNIT], F32, name="zt")
                    acc = bank[:].rearrange("p (j e) -> p j e", j=TILES)
                else:
                    acc = acc_pool.tile([P, TILES, E], F32, name="acc%d" % w)
                for j in range(units[u][2]):
                    rows = slice(j * P, (j + 1) * P)
                    for g in range(PASSES):
                        nc.tensor.matmul_mx(
                            out=acc[:, j, :],
                            lhsT=h["codes"][:, g, rows].bitcast(FP8X4),
                            lhsT_scale=h["scales"][:, g, rows],
                            rhs=w_codes[:, w, g, :].bitcast(FP8X4),
                            rhs_scale=w_scales[:, w, g, :],
                            start=(g == 0),
                            stop=(g == PASSES - 1),
                        )
                acc_tiles[u].append(acc)

        def finish(u):
            block, first, tiles = units[u]
            result_tile = o_pool.tile([P, 3 * HEADS * TILES * HEAD_DIM], F32, name="result")
            result = result_tile[:, : 3 * HEADS * tiles * HEAD_DIM].rearrange(
                "p (w a j d) -> p w a j d", w=3, a=HEADS, j=tiles
            )
            for w, acc in enumerate(acc_tiles[u]):
                nc.vector.tensor_tensor(
                    out=result[:, w].rearrange("p a j d -> p j a d"),
                    in0=acc[:, :tiles].rearrange("p j (a d) -> p j a d", a=HEADS),
                    in1=bias[:, w].to_broadcast([P, tiles, HEADS, HEAD_DIM]),
                    op=ALU.add,
                )
                nc.sync.dma_start(
                    out=out_units[w][block // BLOCKS_PER_BATCH, block % BLOCKS_PER_BATCH][
                        :, :, first * HEAD_DIM : (first + tiles) * HEAD_DIM
                    ],
                    in_=result[:, w].rearrange("p a j d -> p a (j d)"),
                )

        def run(stage, u, *rest):
            if 0 <= u < UNITS:
                stage(u, *rest)

        with tc.manual_schedule():
            load(0)
            load(1)
            spread = start_constants()
            for s in range(UNITS + AHEAD + 2):
                run(load, s + 2)
                if s < len(weights):
                    load_weight(s)
                run(quantise, s - AHEAD - 1)
                run(regroup_on_vector, s - AHEAD)
                run(negate_mean, s - 1)
                run(normalise, s - 1)
                run(finish, s - AHEAD - 2)
                if s == 1:
                    cast_affine()
                if s == AHEAD:
                    cast_bias(spread)
                run(row_statistics, s)
                run(transpose_and_scale, s - 2, 1)
                run(regroup_on_tensor, s - 3)
                run(normalise_on_scalar, s - 1)
                run(transpose_and_scale, s - 2, 0)
                run(row_scalars, s)
                run(regroup_on_scalar, s - 2)
                run(project, s - AHEAD - 1)
